import numpy as np
import ml_dtypes


def mxq(x, axis, fmt="e4m3"):
    dtype, down = {"e4m3": (ml_dtypes.float8_e4m3fn, 7), "e5m2": (ml_dtypes.float8_e5m2, 14)}[fmt]
    v = np.moveaxis(np.asarray(x, np.float32).astype(ml_dtypes.bfloat16).astype(np.float64), axis, -1)
    blocks = v.reshape(v.shape[:-1] + (-1, 32))
    amax = np.abs(blocks).max(-1, keepdims=True)
    byte = np.maximum(np.where(amax > 0, np.frexp(amax)[1] - 1 + 127, 0) - down, 1)
    scale = np.exp2(byte - 127.0)
    codes = (blocks / scale).astype(np.float32).astype(dtype).astype(np.float64)
    return np.moveaxis((codes * scale).reshape(v.shape), -1, axis)


WIDE = False


def mx_kscale(k):
    if not WIDE:
        return np.ones(k)
    levels = np.array([10, -10, 5, -5, 0])
    a = np.random.permutation(np.resize(levels, k // 512 * 4)).reshape(k // 512, 4)
    idx = np.arange(k)
    return np.exp2(a[idx // 512, idx % 128 // 32])


BF16 = ml_dtypes.bfloat16


def bf(x):
    return np.asarray(x, np.float32).astype(BF16)


def f64(x):
    return np.asarray(x).astype(np.float64)


E2M1 = np.array([0.0, 0.5, 1.0, 1.5, 2.0, 3.0, 4.0, 6.0, -0.0, -0.5, -1.0, -1.5, -2.0, -3.0, -4.0, -6.0])


def pack_weight(w, fmt):
    k, n = w.shape
    w = f64(bf(w)).reshape(k // 32, 32, n)
    amax = np.abs(w).max(1)
    if fmt == "e4m3":
        byte = np.frexp(amax)[1] - 1 + 127 - 7
    else:
        mant, ex = np.frexp(amax / 6.0)
        byte = np.where(mant > 0.5, ex, ex - 1) + 127
    byte = np.clip(np.where(amax > 0, byte, 1), 1, 254)
    scaled = (w * np.exp2(127.0 - byte)[:, None, :]).reshape(k, n).astype(np.float32)
    by_word = np.ascontiguousarray(scaled.reshape(k // 512, 128, 4, n).transpose(0, 1, 3, 2))
    if fmt == "e4m3":
        words = by_word.astype(ml_dtypes.float8_e4m3fn).view(np.uint8)
    else:
        c = by_word.astype(ml_dtypes.float4_e2m1fn).view(np.uint8) & 0xF
        words = c[..., 0::2] | (c[..., 1::2] << 4)
    return np.ascontiguousarray(words), np.ascontiguousarray(byte.astype(np.uint8).reshape(k // 512, 16, n))


def unpack_weight(words, scales, fmt):
    g, p, n, _ = words.shape
    if fmt == "e4m3":
        vals = np.ascontiguousarray(words).view(ml_dtypes.float8_e4m3fn).astype(np.float64)
    else:
        nib = np.empty((g, p, n, 4), np.uint8)
        nib[..., 0::2] = words & 0xF
        nib[..., 1::2] = words >> 4
        vals = E2M1[nib]
    vals = vals * np.repeat(np.exp2(scales.astype(np.float64) - 127.0), 8, axis=1)[..., None]
    return vals.transpose(0, 1, 3, 2).reshape(g * 512, n)

def pack4(w):
    words, scales = pack_weight(w, "e2m1")
    return words.reshape(words.shape[0], 128, -1), scales


def unpack4(words, scales):
    return unpack_weight(words.reshape(words.shape[0], 128, -1, 2), scales, "e2m1")


B, T, HS, WS, G, K, CB, CB2, CB3, CB4 = 2, 32, 2, 2, 8, 512, 128, 160, 200, 250
EPS = 1e-3
NV = 5
R = B * T * HS * WS


def bn_apply(v, p):
    gamma, beta, mean, var = p[0], p[1], p[2], p[3]
    return (v - mean) * (gamma / np.sqrt(var + EPS)) + beta


def dwconv_t(v, taps, d):
    vp = np.pad(v, ((0, 0), (d, d), (0, 0), (0, 0), (0, 0), (0, 0)))
    return taps[0] * vp[:, 0:T] + taps[1] * vp[:, d:d + T] + taps[2] * vp[:, 2 * d:2 * d + T]


def setup_inputs():
    s = mx_kscale(K)
    gamma = 1.0 + 0.1 * np.random.standard_normal((NV, G, CB))
    beta = 0.2 * np.random.standard_normal((NV, G, CB))
    mean = 0.04 * np.random.standard_normal((NV, G, CB))
    var = np.random.uniform(0.01, 0.04, (NV, G, CB))
    x = bf(np.random.standard_normal((B, T, HS, WS, G * K)) * np.tile(s, G))
    stack = np.random.standard_normal((NV, G, K, CB)) * 0.15 / np.sqrt(K) / s[:, None]
    words, scales = pack4(stack.reshape(-1, CB))
    return {"x": x,
            "w_words": words,
            "w_scales": scales,
            "b": bf(np.random.standard_normal((NV, G, CB)) * 0.04),
            "dw": bf(np.random.standard_normal((3, 3, G, CB)) * 0.6),
            "bn": bf(np.stack([gamma, beta, mean, var], axis=1))}


def reference(x, w_words, w_scales, b, dw, bn):
    b, dw, bn = f64(b), f64(dw), f64(bn)
    xg = f64(x).reshape(R, G, K).transpose(1, 0, 2)
    wg = unpack4(w_words, w_scales).reshape(NV, G, K, CB).transpose(1, 2, 0, 3).reshape(G, K, NV * CB)
    y = mxq(xg, 2, "e4m3") @ wg
    y = y.reshape(G, B, T, HS, WS, NV, CB).transpose(5, 1, 2, 3, 4, 0, 6) + b[:, None, None, None, None]
    outs = [bn_apply(y[0], bn[0])]
    for i, d in enumerate((1, 2, 3)):
        outs.append(bn_apply(dwconv_t(y[1 + i], dw[i], d), bn[1 + i]))
    t5 = np.maximum(y[4], np.concatenate([y[4][:, 1:], y[4][:, -1:]], axis=1))
    outs.append(bn_apply(t5, bn[4]))
    z = np.stack(outs, axis=5)
    z = np.maximum(z.reshape(B, T, HS, WS, G * NV * CB), 0.0)
    z = z.reshape(B, T, HS, WS, G, NV * CB).swapaxes(-1, -2).reshape(B, T, HS, WS, G * NV * CB)
    return z.reshape(B, T // 2, 2, HS, WS, G * NV * CB).max(axis=2)

@@ -1,0 +1,242 @@
+from contextlib import ExitStack
+
+import concourse.mybir as mybir
+from concourse.masks import make_identity
+
+F32 = mybir.dt.float32
+BF16 = mybir.dt.bfloat16
+I32 = mybir.dt.int32
+U32 = mybir.dt.uint32
+U8 = mybir.dt.uint8
+FP8X4 = mybir.dt.float8_e4m3fn_x4
+FP4X4 = mybir.dt.float4_e2m1fn_x4
+ALU = mybir.AluOpType
+ACT = mybir.ActivationFunctionType
+
+P = 128
+NB = 2
+T = 32
+S = 4
+G = 8
+K = 512
+NV = 5
+EPS = 1e-3
+COLS = T * S
+ROWS = NB * COLS
+HALF = G // 2
+
+BRANCH_ORDER = (1, 2, 3, 4, 0)
+
+FLOPS = 2 * ROWS * K * P * NV * G
+
+
+def tile_timeception_pa_e_kernel(tc, x, w_words, w_scales, b, dw, bn, out):
+    nc = tc.nc
+    with ExitStack() as ctx:
+        keep = ctx.enter_context(tc.tile_pool(name="keep", bufs=1))
+        stage = ctx.enter_context(tc.tile_pool(name="stage", bufs=2))
+        psum_t = ctx.enter_context(tc.psum_pool(name="psum_t", bufs=2))
+        psum_y = ctx.enter_context(tc.psum_pool(name="psum_y", bufs=4))
+        psum_o = ctx.enter_context(tc.psum_pool(name="psum_o", bufs=2))
+
+        w_planes = keep.tile([P, NV * G, P], U8, align_bytes=64)
+        nc.vector.memset(w_planes[:].bitcast(I32), 0)
+
+        x_rows = x.rearrange("n t p q c -> n (t p q) c")
+        x_sb = [keep.tile([P, G * K], BF16, name="x_sb%d" % n) for n in range(NB)]
+
+        def load_x(pair):
+            cols = slice(2 * K * pair, 2 * K * (pair + 1))
+            for n in range(NB):
+                nc.sync.dma_start(out=x_sb[n][:, cols], in_=x_rows[n, :, cols])
+
+        w_sb = keep.tile([P, NV * G, 2 * P], U8, align_bytes=64)
+        words_dram = w_words.bitcast(I32)
+
+        def load_weights(v):
+            mats = slice(G * v, G * (v + 1))
+            nc.sync.dma_start(
+                out=w_sb[:, mats, :].bitcast(I32),
+                in_=words_dram[mats].rearrange("e p c -> p e c"),
+            )
+
+        scales_dram = w_scales.bitcast(I32)
+
+        def load_scales():
+            for q in range(8):
+                first = 32 * (q // 4) + q % 4
+                nc.sync.dma_start(
+                    out=w_planes[first:P:64, :, :].bitcast(I32),
+                    in_=scales_dram[:, q:16:8, :].rearrange("e q c -> q e c"),
+                )
+
+        load_x(0)
+        load_scales()
+        load_weights(BRANCH_ORDER[0])
+        for pair in range(1, G // 2):
+            load_x(pair)
+        for v in BRANCH_ORDER[1:]:
+            load_weights(v)
+
+        ident = keep.tile([P, P], F32)
+        make_identity(nc, ident[:])
+        ident_bf = keep.tile([P, P], BF16)
+        make_identity(nc, ident_bf[:])
+
+        one = keep.tile([P, 1], F32)
+        nc.vector.memset(one[:], 1.0)
+        nc.scalar.activation(out=one[:], in_=one[:], func=ACT.Sqrt)
+
+        rows = keep.tile([P, 3, P], BF16)
+        nc.vector.memset(rows[:, 1:3, :], 0.0)
+        bn_rows = bn.rearrange("v j g o -> (v j g) o")
+        nc.scalar.dma_start(out=rows[:, 0, :], in_=bn_rows[0:P])
+        nc.scalar.dma_start(out=rows[0:32, 1, :], in_=bn_rows[P : P + 32])
+        nc.scalar.dma_start(out=rows[32:72, 1, :], in_=b.rearrange("v g o -> (v g) o"))
+        nc.scalar.dma_start(out=rows[0:72, 2, :], in_=dw.rearrange("i j g o -> (i j g) o"))
+        par_ps = psum_t.tile([P, 3, P], BF16, tag="xt")
+        for c in range(3):
+            nc.tensor.transpose(par_ps[:, c, :], rows[:, c, :], ident_bf[:])
+        par = keep.tile([P, 3 * P], F32)
+        nc.vector.tensor_copy(out=par[:], in_=par_ps[:].rearrange("p c r -> p (c r)"))
+
+        bn_par = par[:, 0 : NV * 4 * G].rearrange("p (v j g) -> p v j g", v=NV, j=4)
+        gamma, beta, mean, var = (
+            bn_par[:, :, 0, :],
+            bn_par[:, :, 1, :],
+            bn_par[:, :, 2, :],
+            bn_par[:, :, 3, :],
+        )
+        bias = par[:, 160:200].rearrange("p (v g) -> p v g", v=NV)
+        dw_par = par[:, 256:328].rearrange("p (i j g) -> p i j g", i=3, j=3)
+
+        scale = keep.tile([P, NV, G], F32)
+        nc.vector.tensor_scalar_add(out=scale[:], in0=var, scalar1=EPS)
+        nc.scalar.activation(out=scale[:], in_=scale[:], func=ACT.Sqrt)
+        nc.vector.reciprocal(out=scale[:], in_=scale[:])
+        nc.vector.tensor_mul(out=scale[:], in0=scale[:], in1=gamma)
+        shift = keep.tile([P, NV, G], F32)
+        nc.vector.tensor_mul(out=shift[:], in0=mean, in1=scale[:])
+        nc.vector.tensor_sub(out=shift[:], in0=beta, in1=shift[:])
+        offset = keep.tile([P, NV, G], F32)
+        nc.vector.tensor_mul(out=offset[:], in0=bias, in1=scale[:])
+        nc.vector.tensor_add(out=offset[:], in0=offset[:], in1=shift[:])
+        spread = [P, 3, 3, G]
+        taps = keep.tile(spread, F32)
+        nc.vector.tensor_mul(
+            out=taps[:], in0=dw_par, in1=scale[:, 1:4, :].unsqueeze(2).to_broadcast(spread)
+        )
+        tap_bias = keep.tile(spread, F32)
+        nc.vector.tensor_mul(
+            out=tap_bias[:], in0=taps[:], in1=bias[:, 1:4, :].unsqueeze(2).to_broadcast(spread)
+        )
+        conv_offset = keep.tile([P, 3, G], F32)
+        nc.vector.tensor_add(out=conv_offset[:], in0=tap_bias[:, :, 0, :], in1=tap_bias[:, :, 1, :])
+        nc.vector.tensor_add(out=conv_offset[:], in0=conv_offset[:], in1=tap_bias[:, :, 2, :])
+        nc.vector.tensor_add(out=conv_offset[:], in0=conv_offset[:], in1=shift[:, 1:4, :])
+
+        x_codes = keep.tile([P, G, ROWS], U32, align_bytes=64)
+        x_planes = keep.tile([P, G, ROWS], U8, align_bytes=64)
+
+        def quantise_group(g):
+            xt = psum_t.tile([P, 2, ROWS], F32, tag="xt")
+            for n in range(NB):
+                words = x_sb[n][:].bitcast(F32)
+                for u in range(2):
+                    nc.tensor.transpose(
+                        xt[:, u, COLS * n : COLS * (n + 1)],
+                        words[:, (K // 2) * g + u : (K // 2) * (g + 1) : 2],
+                        ident[:],
+                    )
+            grouped = stage.tile([P, ROWS * 4], BF16, align_bytes=64)
+            nc.scalar.copy(
+                out=grouped[:].bitcast(F32).rearrange("p (r u) -> p r u", u=2),
+                in_=xt[:].rearrange("p u r -> p r u"),
+            )
+            nc.vector.quantize_mx(
+                out=x_codes[:, g, :].bitcast(FP8X4), scales=x_planes[:, g, :], in_=grouped[:]
+            )
+
+        def branch_group(v, g, z):
+            e = G * v + g
+            y = psum_y.tile([P, ROWS], F32)
+            nc.tensor.matmul_mx(
+                out=y[:],
+                lhsT=w_sb[:, e, :].bitcast(FP4X4),
+                lhsT_scale=w_planes[:, e, :],
+                rhs=x_codes[:, g, :].bitcast(FP8X4),
+                rhs_scale=x_planes[:, g, :],
+                start=True,
+                stop=True,
+            )
+            zg = z[:, g, :]
+            y_nt = y[:].rearrange("p (n c) -> p n c", n=NB)
+            z_nt = zg.rearrange("p (n c) -> p n c", n=NB)
+            if v == 0:
+                nc.scalar.activation(
+                    out=zg, in_=y[:], func=ACT.Identity,
+                    scale=scale[:, v, g : g + 1], bias=offset[:, v, g : g + 1],
+                )
+            elif v == 4:
+                nc.scalar.copy(out=zg, in_=y[:])
+                nc.vector.tensor_max(
+                    out=z_nt[:, :, : COLS - S], in0=z_nt[:, :, : COLS - S], in1=y_nt[:, :, S:]
+                )
+                nc.scalar.activation(
+                    out=zg, in_=zg, func=ACT.Identity,
+                    scale=scale[:, v, g : g + 1], bias=offset[:, v, g : g + 1],
+                )
+            else:
+                i = v - 1
+                w = v * S
+                nc.scalar.activation(
+                    out=zg, in_=y[:], func=ACT.Identity,
+                    scale=taps[:, i, 1, g : g + 1], bias=conv_offset[:, i, g : g + 1],
+                )
+                nc.vector.scalar_tensor_tensor(
+                    out=z_nt[:, :, w:], in0=y_nt[:, :, : COLS - w], scalar=taps[:, i, 0, g : g + 1],
+                    in1=z_nt[:, :, w:], op0=ALU.mult, op1=ALU.add,
+                )
+                nc.vector.scalar_tensor_tensor(
+                    out=z_nt[:, :, : COLS - w], in0=y_nt[:, :, w:], scalar=taps[:, i, 2, g : g + 1],
+                    in1=z_nt[:, :, : COLS - w], op0=ALU.mult, op1=ALU.add,
+                )
+
+        def finish_half(v, h, z, result):
+            groups = slice(HALF * h, HALF * (h + 1))
+            if 1 <= v <= 3:
+                w = v * S
+                edge = [P, HALF, NB, w]
+                z_edges = z[:, groups, :].rearrange("p g (n c) -> p g n c", n=NB)
+                for j, cols in ((0, slice(0, w)), (2, slice(COLS - w, COLS))):
+                    nc.vector.tensor_sub(
+                        out=z_edges[:, :, :, cols],
+                        in0=z_edges[:, :, :, cols],
+                        in1=tap_bias[:, v - 1, j, groups].unsqueeze(2).unsqueeze(3).to_broadcast(edge),
+                    )
+            pairs = z[:, groups, :].rearrange("p g (m two s) -> p (g m) two s", two=2, s=S)
+            pooled = stage.tile([P, HALF, COLS], F32)
+            nc.vector.scalar_tensor_tensor(
+                out=pooled[:].rearrange("p g (m s) -> p (g m) s", s=S),
+                in0=pairs[:, :, 0, :], scalar=0.0, in1=pairs[:, :, 1, :],
+                op0=ALU.max, op1=ALU.max,
+            )
+            turned = psum_o.tile([P, HALF, P], F32)
+            for j in range(HALF):
+                nc.tensor.transpose(turned[:, j, :], pooled[:, j, :], ident[:])
+            nc.scalar.copy(out=result[:, :, groups], in_=turned[:].rearrange("p g o -> p o g"))
+
+        out_rows = out.rearrange("n t p q c -> (n t p q) c")
+        for v in BRANCH_ORDER:
+            z = stage.tile([P, G, ROWS], F32)
+            result = stage.tile([P, P, G], F32)
+            for h in range(2):
+                for g in range(HALF * h, HALF * (h + 1)):
+                    if v == BRANCH_ORDER[0]:
+                        quantise_group(g)
+                    branch_group(v, g, z)
+                finish_half(v, h, z, result)
+            nc.sync.dma_start(
+                out=out_rows[:, P * G * v : P * G * (v + 1)],
+                in_=result[:].rearrange("p o g -> p (o g)"),
+            )

@@ -23,24 +23,65 @@ NV = 5
 EPS = 1e-3
 COLS = T * S
 ROWS = NB * COLS
+PAIRS = G // 2
 HALF = G // 2
 
-BRANCH_ORDER = (1, 2, 3, 4, 0)
+CONV = (3, 2, 1)
+OTHER = (4, 0)
+FIRST_WEIGHTS = slice(3 * G, 5 * G)
+LATER_WEIGHTS = slice(0, 3 * G)
 
 FLOPS = 2 * ROWS * K * P * NV * G
+
+
+def work_order():
+    conv = [(v, pair) for v in CONV for pair in range(PAIRS)]
+    other = [(v, pair) for v in OTHER for pair in range(PAIRS)]
+    steps = []
+    for i in range(len(conv)):
+        steps.append(conv[i])
+        if i < len(other):
+            steps.append(other[i])
+    return steps
 
 
 def tile_timeception_pa_e_kernel(tc, x, w_words, w_scales, b, dw, bn, out):
     nc = tc.nc
     with ExitStack() as ctx:
+        ctx.enter_context(tc.manual_schedule())
         keep = ctx.enter_context(tc.tile_pool(name="keep", bufs=1))
         stage = ctx.enter_context(tc.tile_pool(name="stage", bufs=2))
+        branch = ctx.enter_context(tc.tile_pool(name="branch", bufs=4))
         psum_t = ctx.enter_context(tc.psum_pool(name="psum_t", bufs=2))
         psum_y = ctx.enter_context(tc.psum_pool(name="psum_y", bufs=4))
         psum_o = ctx.enter_context(tc.psum_pool(name="psum_o", bufs=2))
 
+        one = keep.tile([P, 1], F32)
+        nc.vector.memset(one[:], 1.0)
+        rows = keep.tile([P, 3, P], BF16)
+        nc.vector.memset(rows[:, 1:3, :], 0.0)
+        bn_rows = bn.rearrange("v j g o -> (v j g) o")
+        nc.scalar.dma_start(out=rows[:, 0, :], in_=bn_rows[0:P])
+        nc.scalar.dma_start(out=rows[0:32, 1, :], in_=bn_rows[P : P + 32])
+        nc.scalar.dma_start(out=rows[32:72, 1, :], in_=b.rearrange("v g o -> (v g) o"))
+        nc.scalar.dma_start(out=rows[0:72, 2, :], in_=dw.rearrange("i j g o -> (i j g) o"))
+
         w_planes = keep.tile([P, NV * G, P], U8, align_bytes=64)
         nc.vector.memset(w_planes[:].bitcast(I32), 0)
+        w_sb = keep.tile([P, NV * G, 2 * P], U8, align_bytes=64)
+        words_dram = w_words.bitcast(I32)
+        scales_dram = w_scales.bitcast(I32)
+
+        def load_weights(mats):
+            for r in range(4):
+                nc.sync.dma_start(
+                    out=w_planes[r:P:32, mats, :].bitcast(I32),
+                    in_=scales_dram[mats, r:16:4, :].rearrange("e q c -> q e c"),
+                )
+            nc.sync.dma_start(
+                out=w_sb[:, mats, :].bitcast(I32),
+                in_=words_dram[mats].rearrange("e p c -> p e c"),
+            )
 
         x_rows = x.rearrange("n t p q c -> n (t p q) c")
         x_sb = [keep.tile([P, G * K], BF16, name="x_sb%d" % n) for n in range(NB)]
@@ -50,50 +91,19 @@ def tile_timeception_pa_e_kernel(tc, x, w_words, w_scales, b, dw, bn, out):
             for n in range(NB):
                 nc.sync.dma_start(out=x_sb[n][:, cols], in_=x_rows[n, :, cols])
 
-        w_sb = keep.tile([P, NV * G, 2 * P], U8, align_bytes=64)
-        words_dram = w_words.bitcast(I32)
-
-        def load_weights(v):
-            mats = slice(G * v, G * (v + 1))
-            nc.sync.dma_start(
-                out=w_sb[:, mats, :].bitcast(I32),
-                in_=words_dram[mats].rearrange("e p c -> p e c"),
-            )
-
-        scales_dram = w_scales.bitcast(I32)
-
-        def load_scales():
-            for q in range(8):
-                first = 32 * (q // 4) + q % 4
-                nc.sync.dma_start(
-                    out=w_planes[first:P:64, :, :].bitcast(I32),
-                    in_=scales_dram[:, q:16:8, :].rearrange("e q c -> q e c"),
-                )
-
         load_x(0)
-        load_scales()
-        load_weights(BRANCH_ORDER[0])
-        for pair in range(1, G // 2):
+        load_weights(FIRST_WEIGHTS)
+        for pair in range(1, PAIRS):
             load_x(pair)
-        for v in BRANCH_ORDER[1:]:
-            load_weights(v)
+        load_weights(LATER_WEIGHTS)
 
-        ident = keep.tile([P, P], F32)
-        make_identity(nc, ident[:])
         ident_bf = keep.tile([P, P], BF16)
         make_identity(nc, ident_bf[:])
+        ident = keep.tile([P, P], F32)
+        make_identity(nc, ident[:])
 
-        one = keep.tile([P, 1], F32)
-        nc.vector.memset(one[:], 1.0)
         nc.scalar.activation(out=one[:], in_=one[:], func=ACT.Sqrt)
 
-        rows = keep.tile([P, 3, P], BF16)
-        nc.vector.memset(rows[:, 1:3, :], 0.0)
-        bn_rows = bn.rearrange("v j g o -> (v j g) o")
-        nc.scalar.dma_start(out=rows[:, 0, :], in_=bn_rows[0:P])
-        nc.scalar.dma_start(out=rows[0:32, 1, :], in_=bn_rows[P : P + 32])
-        nc.scalar.dma_start(out=rows[32:72, 1, :], in_=b.rearrange("v g o -> (v g) o"))
-        nc.scalar.dma_start(out=rows[0:72, 2, :], in_=dw.rearrange("i j g o -> (i j g) o"))
         par_ps = psum_t.tile([P, 3, P], BF16, tag="xt")
         for c in range(3):
             nc.tensor.transpose(par_ps[:, c, :], rows[:, c, :], ident_bf[:])
@@ -101,12 +111,10 @@ def tile_timeception_pa_e_kernel(tc, x, w_words, w_scales, b, dw, bn, out):
         nc.vector.tensor_copy(out=par[:], in_=par_ps[:].rearrange("p c r -> p (c r)"))
 
         bn_par = par[:, 0 : NV * 4 * G].rearrange("p (v j g) -> p v j g", v=NV, j=4)
-        gamma, beta, mean, var = (
-            bn_par[:, :, 0, :],
-            bn_par[:, :, 1, :],
-            bn_par[:, :, 2, :],
-            bn_par[:, :, 3, :],
-        )
+        gamma = bn_par[:, :, 0, :]
+        beta = bn_par[:, :, 1, :]
+        mean = bn_par[:, :, 2, :]
+        var = bn_par[:, :, 3, :]
         bias = par[:, 160:200].rearrange("p (v g) -> p v g", v=NV)
         dw_par = par[:, 256:328].rearrange("p (i j g) -> p i j g", i=3, j=3)
 
@@ -137,106 +145,201 @@ def tile_timeception_pa_e_kernel(tc, x, w_words, w_scales, b, dw, bn, out):
 
         x_codes = keep.tile([P, G, ROWS], U32, align_bytes=64)
         x_planes = keep.tile([P, G, ROWS], U8, align_bytes=64)
+        x_turned = {}
+        x_grouped = {}
 
-        def quantise_group(g):
-            xt = psum_t.tile([P, 2, ROWS], F32, tag="xt")
-            for n in range(NB):
-                words = x_sb[n][:].bitcast(F32)
-                for u in range(2):
-                    nc.tensor.transpose(
-                        xt[:, u, COLS * n : COLS * (n + 1)],
-                        words[:, (K // 2) * g + u : (K // 2) * (g + 1) : 2],
-                        ident[:],
-                    )
-            grouped = stage.tile([P, ROWS * 4], BF16, align_bytes=64)
-            nc.scalar.copy(
-                out=grouped[:].bitcast(F32).rearrange("p (r u) -> p r u", u=2),
-                in_=xt[:].rearrange("p u r -> p r u"),
-            )
+        def transpose_x(pair):
+            for g in (2 * pair, 2 * pair + 1):
+                xt = psum_t.tile([P, 2, ROWS], F32, tag="xt")
+                x_turned[g] = xt
+                for n in range(NB):
+                    words = x_sb[n][:].bitcast(F32)
+                    for u in range(2):
+                        nc.tensor.transpose(
+                            xt[:, u, COLS * n : COLS * (n + 1)],
+                            words[:, (K // 2) * g + u : (K // 2) * (g + 1) : 2],
+                            ident[:],
+                        )
+
+        def regroup_x(pair):
+            grouped = stage.tile([P, 2, ROWS * 4], BF16, align_bytes=64)
+            x_grouped[pair] = grouped
+            for i in range(2):
+                g = 2 * pair + i
+                together = grouped[:, i, :].bitcast(F32).rearrange("p (r u) -> p r u", u=2)
+                planes = x_turned[g][:].rearrange("p u r -> p r u")
+                if g == 0:
+                    nc.vector.tensor_copy(out=together, in_=planes)
+                else:
+                    nc.scalar.copy(out=together, in_=planes)
+
+        def quantise_x(pair):
+            both = slice(2 * pair, 2 * pair + 2)
             nc.vector.quantize_mx(
-                out=x_codes[:, g, :].bitcast(FP8X4), scales=x_planes[:, g, :], in_=grouped[:]
+                out=x_codes[:, both, :].rearrange("p g r -> p (g r)").bitcast(FP8X4),
+                scales=x_planes[:, both, :].rearrange("p g r -> p (g r)"),
+                in_=x_grouped[pair][:].rearrange("p i c -> p (i c)"),
             )
 
-        def branch_group(v, g, z):
-            e = G * v + g
-            y = psum_y.tile([P, ROWS], F32)
-            nc.tensor.matmul_mx(
-                out=y[:],
-                lhsT=w_sb[:, e, :].bitcast(FP4X4),
-                lhsT_scale=w_planes[:, e, :],
-                rhs=x_codes[:, g, :].bitcast(FP8X4),
-                rhs_scale=x_planes[:, g, :],
-                start=True,
-                stop=True,
-            )
-            zg = z[:, g, :]
-            y_nt = y[:].rearrange("p (n c) -> p n c", n=NB)
-            z_nt = zg.rearrange("p (n c) -> p n c", n=NB)
-            if v == 0:
-                nc.scalar.activation(
-                    out=zg, in_=y[:], func=ACT.Identity,
-                    scale=scale[:, v, g : g + 1], bias=offset[:, v, g : g + 1],
+        steps = work_order()
+        y_tiles = {}
+        z_tiles = {}
+        results = {}
+        pooled_tiles = {}
+        turned_tiles = {}
+
+        def by_batch(ap):
+            return ap.rearrange("p (n c) -> p n c", n=NB)
+
+        def multiply(j):
+            v, pair = steps[j]
+            y = psum_y.tile([P, 2, ROWS], F32)
+            y_tiles[j] = y
+            for i in range(2):
+                g = 2 * pair + i
+                nc.tensor.matmul_mx(
+                    out=y[:, i, :],
+                    lhsT=w_sb[:, G * v + g, :].bitcast(FP4X4),
+                    lhsT_scale=w_planes[:, G * v + g, :],
+                    rhs=x_codes[:, g, :].bitcast(FP8X4),
+                    rhs_scale=x_planes[:, g, :],
+                    start=True,
+                    stop=True,
                 )
-            elif v == 4:
-                nc.scalar.copy(out=zg, in_=y[:])
+
+        def leave_psum(j):
+            v, pair = steps[j]
+            if pair == 0:
+                z = branch.tile([P, G, ROWS], F32)
+                z_tiles[v] = z
+            for i in range(2):
+                g = 2 * pair + i
+                zg = z_tiles[v][:, g, :]
+                yg = y_tiles[j][:, i, :]
+                if v == 0:
+                    nc.scalar.activation(
+                        out=zg, in_=yg, func=ACT.Identity,
+                        scale=scale[:, v, g : g + 1], bias=offset[:, v, g : g + 1],
+                    )
+                elif v == 4:
+                    nc.scalar.copy(out=zg, in_=yg)
+                else:
+                    nc.scalar.activation(
+                        out=zg, in_=yg, func=ACT.Identity,
+                        scale=taps[:, v - 1, 1, g : g + 1], bias=conv_offset[:, v - 1, g : g + 1],
+                    )
+
+        def add_tap(j, tap):
+            v, pair = steps[j]
+            w = v * S
+            for i in range(2):
+                g = 2 * pair + i
+                z_nt = by_batch(z_tiles[v][:, g, :])
+                y_nt = by_batch(y_tiles[j][:, i, :])
+                if tap == 0:
+                    target, source = z_nt[:, :, w:], y_nt[:, :, : COLS - w]
+                else:
+                    target, source = z_nt[:, :, : COLS - w], y_nt[:, :, w:]
+                nc.vector.scalar_tensor_tensor(
+                    out=target, in0=source, scalar=taps[:, v - 1, tap, g : g + 1], in1=target,
+                    op0=ALU.mult, op1=ALU.add,
+                )
+
+        def max_with_next(j):
+            v, pair = steps[j]
+            for i in range(2):
+                z_nt = by_batch(z_tiles[v][:, 2 * pair + i, :])
+                y_nt = by_batch(y_tiles[j][:, i, :])
                 nc.vector.tensor_max(
                     out=z_nt[:, :, : COLS - S], in0=z_nt[:, :, : COLS - S], in1=y_nt[:, :, S:]
                 )
+
+        def normalise(j):
+            v, pair = steps[j]
+            for g in (2 * pair, 2 * pair + 1):
                 nc.scalar.activation(
-                    out=zg, in_=zg, func=ACT.Identity,
+                    out=z_tiles[v][:, g, :], in_=z_tiles[v][:, g, :], func=ACT.Identity,
                     scale=scale[:, v, g : g + 1], bias=offset[:, v, g : g + 1],
                 )
-            else:
-                i = v - 1
-                w = v * S
-                nc.scalar.activation(
-                    out=zg, in_=y[:], func=ACT.Identity,
-                    scale=taps[:, i, 1, g : g + 1], bias=conv_offset[:, i, g : g + 1],
-                )
-                nc.vector.scalar_tensor_tensor(
-                    out=z_nt[:, :, w:], in0=y_nt[:, :, : COLS - w], scalar=taps[:, i, 0, g : g + 1],
-                    in1=z_nt[:, :, w:], op0=ALU.mult, op1=ALU.add,
-                )
-                nc.vector.scalar_tensor_tensor(
-                    out=z_nt[:, :, : COLS - w], in0=y_nt[:, :, w:], scalar=taps[:, i, 2, g : g + 1],
-                    in1=z_nt[:, :, : COLS - w], op0=ALU.mult, op1=ALU.add,
+
+        def finished(j):
+            if 0 <= j < len(steps) and steps[j][1] % 2 == 1:
+                return steps[j][0], steps[j][1] // 2
+            return None
+
+        def mend_edges(v, h):
+            groups = slice(HALF * h, HALF * (h + 1))
+            w = v * S
+            z_edges = z_tiles[v][:, groups, :].rearrange("p g (n c) -> p g n c", n=NB)
+            for tap, cols in ((0, slice(0, w)), (2, slice(COLS - w, COLS))):
+                extra = tap_bias[:, v - 1, tap, groups].unsqueeze(2).unsqueeze(3)
+                nc.vector.tensor_sub(
+                    out=z_edges[:, :, :, cols],
+                    in0=z_edges[:, :, :, cols],
+                    in1=extra.to_broadcast([P, HALF, NB, w]),
                 )
 
-        def finish_half(v, h, z, result):
+        def pool_pairs(v, h):
             groups = slice(HALF * h, HALF * (h + 1))
-            if 1 <= v <= 3:
-                w = v * S
-                edge = [P, HALF, NB, w]
-                z_edges = z[:, groups, :].rearrange("p g (n c) -> p g n c", n=NB)
-                for j, cols in ((0, slice(0, w)), (2, slice(COLS - w, COLS))):
-                    nc.vector.tensor_sub(
-                        out=z_edges[:, :, :, cols],
-                        in0=z_edges[:, :, :, cols],
-                        in1=tap_bias[:, v - 1, j, groups].unsqueeze(2).unsqueeze(3).to_broadcast(edge),
-                    )
-            pairs = z[:, groups, :].rearrange("p g (m two s) -> p (g m) two s", two=2, s=S)
+            pairs = z_tiles[v][:, groups, :].rearrange("p g (m two s) -> p (g m) two s", two=2, s=S)
             pooled = stage.tile([P, HALF, COLS], F32)
+            pooled_tiles[v, h] = pooled
             nc.vector.scalar_tensor_tensor(
                 out=pooled[:].rearrange("p g (m s) -> p (g m) s", s=S),
                 in0=pairs[:, :, 0, :], scalar=0.0, in1=pairs[:, :, 1, :],
                 op0=ALU.max, op1=ALU.max,
             )
+
+        def turn(v, h):
             turned = psum_o.tile([P, HALF, P], F32)
-            for j in range(HALF):
-                nc.tensor.transpose(turned[:, j, :], pooled[:, j, :], ident[:])
-            nc.scalar.copy(out=result[:, :, groups], in_=turned[:].rearrange("p g o -> p o g"))
+            turned_tiles[v, h] = turned
+            for i in range(HALF):
+                nc.tensor.transpose(turned[:, i, :], pooled_tiles[v, h][:, i, :], ident[:])
 
         out_rows = out.rearrange("n t p q c -> (n t p q) c")
-        for v in BRANCH_ORDER:
-            z = stage.tile([P, G, ROWS], F32)
-            result = stage.tile([P, P, G], F32)
-            for h in range(2):
-                for g in range(HALF * h, HALF * (h + 1)):
-                    if v == BRANCH_ORDER[0]:
-                        quantise_group(g)
-                    branch_group(v, g, z)
-                finish_half(v, h, z, result)
-            nc.sync.dma_start(
-                out=out_rows[:, P * G * v : P * G * (v + 1)],
-                in_=result[:].rearrange("p o g -> p (o g)"),
+
+        def shuffle_out(v, h):
+            if h == 0:
+                result = branch.tile([P, P, G], F32)
+                results[v] = result
+            nc.scalar.copy(
+                out=results[v][:, :, HALF * h : HALF * (h + 1)],
+                in_=turned_tiles[v, h][:].rearrange("p g o -> p o g"),
             )
+            if h == 1:
+                nc.sync.dma_start(
+                    out=out_rows[:, P * G * v : P * G * (v + 1)],
+                    in_=results[v][:].rearrange("p o g -> p (o g)"),
+                )
+
+        for j in range(-3, len(steps) + 3):
+            now = steps[j] if 0 <= j < len(steps) else None
+            if now is not None and now[0] in CONV:
+                add_tap(j, 0)
+            if now is not None and now[0] == 4:
+                max_with_next(j)
+            if j % 2 == 0 and 0 <= (j + 2) // 2 < PAIRS:
+                quantise_x((j + 2) // 2)
+            if finished(j - 1) is not None and finished(j - 1)[0] in CONV:
+                mend_edges(*finished(j - 1))
+            if finished(j - 2) is not None:
+                pool_pairs(*finished(j - 2))
+
+            if 0 <= j + 2 < len(steps):
+                multiply(j + 2)
+            if j % 2 == 1 and 0 <= (j + 3) // 2 < PAIRS:
+                transpose_x((j + 3) // 2)
+
+            if 0 <= j + 1 < len(steps):
+                leave_psum(j + 1)
+            if j % 2 == 1 and 0 <= (j + 3) // 2 < PAIRS:
+                regroup_x((j + 3) // 2)
+            if now is not None and now[0] == 4:
+                normalise(j)
+            if finished(j - 3) is not None:
+                shuffle_out(*finished(j - 3))
+
+            if now is not None and now[0] in CONV:
+                add_tap(j, 2)
+            if finished(j - 2) is not None:
+                turn(*finished(j - 2))

@@ -28,8 +28,6 @@ HALF = G // 2
 
 CONV = (3, 2, 1)
 OTHER = (4, 0)
-FIRST_WEIGHTS = slice(3 * G, 5 * G)
-LATER_WEIGHTS = slice(0, 3 * G)
 
 FLOPS = 2 * ROWS * K * P * NV * G
 
@@ -37,18 +35,16 @@ FLOPS = 2 * ROWS * K * P * NV * G
 def work_order():
     conv = [(v, pair) for v in CONV for pair in range(PAIRS)]
     other = [(v, pair) for v in OTHER for pair in range(PAIRS)]
-    steps = []
-    for i in range(len(conv)):
-        steps.append(conv[i])
-        if i < len(other):
-            steps.append(other[i])
+    steps = conv[:PAIRS]
+    for i in range(len(other)):
+        steps.append(conv[PAIRS + i])
+        steps.append(other[i])
     return steps
 
 
 def tile_timeception_pa_e_kernel(tc, x, w_words, w_scales, b, dw, bn, out):
     nc = tc.nc
     with ExitStack() as ctx:
-        ctx.enter_context(tc.manual_schedule())
         keep = ctx.enter_context(tc.tile_pool(name="keep", bufs=1))
         stage = ctx.enter_context(tc.tile_pool(name="stage", bufs=2))
         branch = ctx.enter_context(tc.tile_pool(name="branch", bufs=4))
@@ -72,12 +68,16 @@ def tile_timeception_pa_e_kernel(tc, x, w_words, w_scales, b, dw, bn, out):
         words_dram = w_words.bitcast(I32)
         scales_dram = w_scales.bitcast(I32)
 
-        def load_weights(mats):
+        def load_scales(first_branch, last_branch):
+            mats = slice(G * first_branch, G * (last_branch + 1))
             for r in range(4):
                 nc.sync.dma_start(
                     out=w_planes[r:P:32, mats, :].bitcast(I32),
                     in_=scales_dram[mats, r:16:4, :].rearrange("e q c -> q e c"),
                 )
+
+        def load_words(first_branch, last_branch):
+            mats = slice(G * first_branch, G * (last_branch + 1))
             nc.sync.dma_start(
                 out=w_sb[:, mats, :].bitcast(I32),
                 in_=words_dram[mats].rearrange("e p c -> p e c"),
@@ -86,16 +86,21 @@ def tile_timeception_pa_e_kernel(tc, x, w_words, w_scales, b, dw, bn, out):
         x_rows = x.rearrange("n t p q c -> n (t p q) c")
         x_sb = [keep.tile([P, G * K], BF16, name="x_sb%d" % n) for n in range(NB)]
 
-        def load_x(pair):
-            cols = slice(2 * K * pair, 2 * K * (pair + 1))
+        def load_x(first_group, last_group):
+            cols = slice(K * first_group, K * (last_group + 1))
             for n in range(NB):
                 nc.sync.dma_start(out=x_sb[n][:, cols], in_=x_rows[n, :, cols])
 
-        load_x(0)
-        load_weights(FIRST_WEIGHTS)
+        load_x(0, 0)
+        load_scales(3, 4)
+        load_words(3, 3)
+        load_x(1, 1)
         for pair in range(1, PAIRS):
-            load_x(pair)
-        load_weights(LATER_WEIGHTS)
+            load_x(2 * pair, 2 * pair + 1)
+        load_scales(0, 2)
+        load_words(2, 2)
+        load_words(4, 4)
+        load_words(0, 1)
 
         ident_bf = keep.tile([P, P], BF16)
         make_identity(nc, ident_bf[:])
@@ -145,40 +150,23 @@ def tile_timeception_pa_e_kernel(tc, x, w_words, w_scales, b, dw, bn, out):
 
         x_codes = keep.tile([P, G, ROWS], U32, align_bytes=64)
         x_planes = keep.tile([P, G, ROWS], U8, align_bytes=64)
-        x_turned = {}
-        x_grouped = {}
-
-        def transpose_x(pair):
-            for g in (2 * pair, 2 * pair + 1):
-                xt = psum_t.tile([P, 2, ROWS], F32, tag="xt")
-                x_turned[g] = xt
-                for n in range(NB):
-                    words = x_sb[n][:].bitcast(F32)
-                    for u in range(2):
-                        nc.tensor.transpose(
-                            xt[:, u, COLS * n : COLS * (n + 1)],
-                            words[:, (K // 2) * g + u : (K // 2) * (g + 1) : 2],
-                            ident[:],
-                        )
-
-        def regroup_x(pair):
-            grouped = stage.tile([P, 2, ROWS * 4], BF16, align_bytes=64)
-            x_grouped[pair] = grouped
-            for i in range(2):
-                g = 2 * pair + i
-                together = grouped[:, i, :].bitcast(F32).rearrange("p (r u) -> p r u", u=2)
-                planes = x_turned[g][:].rearrange("p u r -> p r u")
-                if g == 0:
-                    nc.vector.tensor_copy(out=together, in_=planes)
-                else:
-                    nc.scalar.copy(out=together, in_=planes)
-
-        def quantise_x(pair):
-            both = slice(2 * pair, 2 * pair + 2)
+        for g in range(G):
+            xt = psum_t.tile([P, 2, ROWS], F32, tag="xt")
+            for n in range(NB):
+                words = x_sb[n][:].bitcast(F32)
+                for u in range(2):
+                    nc.tensor.transpose(
+                        xt[:, u, COLS * n : COLS * (n + 1)],
+                        words[:, (K // 2) * g + u : (K // 2) * (g + 1) : 2],
+                        ident[:],
+                    )
+            grouped = stage.tile([P, ROWS * 4], BF16, align_bytes=64)
+            nc.scalar.copy(
+                out=grouped[:].bitcast(F32).rearrange("p (r u) -> p r u", u=2),
+                in_=xt[:].rearrange("p u r -> p r u"),
+            )
             nc.vector.quantize_mx(
-                out=x_codes[:, both, :].rearrange("p g r -> p (g r)").bitcast(FP8X4),
-                scales=x_planes[:, both, :].rearrange("p g r -> p (g r)"),
-                in_=x_grouped[pair][:].rearrange("p i c -> p (i c)"),
+                out=x_codes[:, g, :].bitcast(FP8X4), scales=x_planes[:, g, :], in_=grouped[:]
             )
 
         steps = work_order()
@@ -312,34 +300,28 @@ def tile_timeception_pa_e_kernel(tc, x, w_words, w_scales, b, dw, bn, out):
                     in_=results[v][:].rearrange("p o g -> p (o g)"),
                 )
 
-        for j in range(-3, len(steps) + 3):
-            now = steps[j] if 0 <= j < len(steps) else None
-            if now is not None and now[0] in CONV:
-                add_tap(j, 0)
-            if now is not None and now[0] == 4:
-                max_with_next(j)
-            if j % 2 == 0 and 0 <= (j + 2) // 2 < PAIRS:
-                quantise_x((j + 2) // 2)
-            if finished(j - 1) is not None and finished(j - 1)[0] in CONV:
-                mend_edges(*finished(j - 1))
-            if finished(j - 2) is not None:
-                pool_pairs(*finished(j - 2))
+        with tc.manual_schedule():
+            for j in range(-2, len(steps) + 5):
+                now = steps[j] if 0 <= j < len(steps) else None
+                if now is not None and now[0] in CONV:
+                    add_tap(j, 0)
+                if now is not None and now[0] == 4:
+                    max_with_next(j)
+                if finished(j - 1) is not None and finished(j - 1)[0] in CONV:
+                    mend_edges(*finished(j - 1))
+                if finished(j - 2) is not None:
+                    pool_pairs(*finished(j - 2))
+                if now is not None and now[0] in CONV:
+                    add_tap(j, 2)
 
-            if 0 <= j + 2 < len(steps):
-                multiply(j + 2)
-            if j % 2 == 1 and 0 <= (j + 3) // 2 < PAIRS:
-                transpose_x((j + 3) // 2)
+                if 0 <= j + 2 < len(steps):
+                    multiply(j + 2)
+                if finished(j - 3) is not None:
+                    turn(*finished(j - 3))
 
-            if 0 <= j + 1 < len(steps):
-                leave_psum(j + 1)
-            if j % 2 == 1 and 0 <= (j + 3) // 2 < PAIRS:
-                regroup_x((j + 3) // 2)
-            if now is not None and now[0] == 4:
-                normalise(j)
-            if finished(j - 3) is not None:
-                shuffle_out(*finished(j - 3))
-
-            if now is not None and now[0] in CONV:
-                add_tap(j, 2)
-            if finished(j - 2) is not None:
-                turn(*finished(j - 2))
+                if 0 <= j + 1 < len(steps):
+                    leave_psum(j + 1)
+                if now is not None and now[0] == 4:
+                    normalise(j)
+                if finished(j - 4) is not None:
+                    shuffle_out(*finished(j - 4))

@@ -245,9 +245,10 @@ def tile_timeception_pa_e_kernel(tc, x, w_words, w_scales, b, dw, bn, out):
         def normalise(j):
             v, pair = steps[j]
             for g in (2 * pair, 2 * pair + 1):
-                nc.scalar.activation(
-                    out=z_tiles[v][:, g, :], in_=z_tiles[v][:, g, :], func=ACT.Identity,
-                    scale=scale[:, v, g : g + 1], bias=offset[:, v, g : g + 1],
+                nc.gpsimd.tensor_scalar(
+                    out=z_tiles[v][:, g, :], in0=z_tiles[v][:, g, :],
+                    scalar1=scale[:, v, g : g + 1], scalar2=offset[:, v, g : g + 1],
+                    op0=ALU.mult, op1=ALU.add,
                 )
 
         def finished(j):
@@ -261,10 +262,11 @@ def tile_timeception_pa_e_kernel(tc, x, w_words, w_scales, b, dw, bn, out):
             z_edges = z_tiles[v][:, groups, :].rearrange("p g (n c) -> p g n c", n=NB)
             for tap, cols in ((0, slice(0, w)), (2, slice(COLS - w, COLS))):
                 extra = tap_bias[:, v - 1, tap, groups].unsqueeze(2).unsqueeze(3)
-                nc.vector.tensor_sub(
+                nc.gpsimd.tensor_tensor(
                     out=z_edges[:, :, :, cols],
                     in0=z_edges[:, :, :, cols],
                     in1=extra.to_broadcast([P, HALF, NB, w]),
+                    op=ALU.subtract,
                 )
 
         def pool_pairs(v, h):

@@ -37,8 +37,8 @@ def work_order():
     other = [(v, pair) for v in OTHER for pair in range(PAIRS)]
     steps = conv[:PAIRS]
     for i in range(len(other)):
-        steps.append(conv[PAIRS + i])
         steps.append(other[i])
+        steps.append(conv[PAIRS + i])
     return steps
 
 
@@ -98,8 +98,8 @@ def tile_timeception_pa_e_kernel(tc, x, w_words, w_scales, b, dw, bn, out):
         for pair in range(1, PAIRS):
             load_x(2 * pair, 2 * pair + 1)
         load_scales(0, 2)
-        load_words(2, 2)
         load_words(4, 4)
+        load_words(2, 2)
         load_words(0, 1)
 
         ident_bf = keep.tile([P, P], BF16)
@@ -200,6 +200,9 @@ def tile_timeception_pa_e_kernel(tc, x, w_words, w_scales, b, dw, bn, out):
             if pair == 0:
                 z = branch.tile([P, G, ROWS], F32)
                 z_tiles[v] = z
+            if v == 4:
+                nc.scalar.copy(out=z_tiles[v][:, 2 * pair : 2 * pair + 2, :], in_=y_tiles[j][:])
+                return
             for i in range(2):
                 g = 2 * pair + i
                 zg = z_tiles[v][:, g, :]
@@ -209,8 +212,6 @@ def tile_timeception_pa_e_kernel(tc, x, w_words, w_scales, b, dw, bn, out):
                         out=zg, in_=yg, func=ACT.Identity,
                         scale=scale[:, v, g : g + 1], bias=offset[:, v, g : g + 1],
                     )
-                elif v == 4:
-                    nc.scalar.copy(out=zg, in_=yg)
                 else:
                     nc.scalar.activation(
                         out=zg, in_=yg, func=ACT.Identity,
@@ -235,12 +236,11 @@ def tile_timeception_pa_e_kernel(tc, x, w_words, w_scales, b, dw, bn, out):
 
         def max_with_next(j):
             v, pair = steps[j]
-            for i in range(2):
-                z_nt = by_batch(z_tiles[v][:, 2 * pair + i, :])
-                y_nt = by_batch(y_tiles[j][:, i, :])
-                nc.vector.tensor_max(
-                    out=z_nt[:, :, : COLS - S], in0=z_nt[:, :, : COLS - S], in1=y_nt[:, :, S:]
-                )
+            z_nt = z_tiles[v][:, 2 * pair : 2 * pair + 2, :].rearrange("p g (n c) -> p (g n) c", n=NB)
+            y_nt = y_tiles[j][:].rearrange("p g (n c) -> p (g n) c", n=NB)
+            nc.vector.tensor_max(
+                out=z_nt[:, :, : COLS - S], in0=z_nt[:, :, : COLS - S], in1=y_nt[:, :, S:]
+            )
 
         def normalise(j):
             v, pair = steps[j]

@@ -48,6 +48,7 @@ def tile_timeception_pa_e_kernel(tc, x, w_words, w_scales, b, dw, bn, out):
         keep = ctx.enter_context(tc.tile_pool(name="keep", bufs=1))
         stage = ctx.enter_context(tc.tile_pool(name="stage", bufs=2))
         branch = ctx.enter_context(tc.tile_pool(name="branch", bufs=4))
+        regrouped = ctx.enter_context(tc.tile_pool(name="regrouped", bufs=4))
         psum_t = ctx.enter_context(tc.psum_pool(name="psum_t", bufs=2))
         psum_y = ctx.enter_context(tc.psum_pool(name="psum_y", bufs=4))
         psum_o = ctx.enter_context(tc.psum_pool(name="psum_o", bufs=2))
@@ -57,10 +58,14 @@ def tile_timeception_pa_e_kernel(tc, x, w_words, w_scales, b, dw, bn, out):
         rows = keep.tile([P, 3, P], BF16)
         nc.vector.memset(rows[:, 1:3, :], 0.0)
         bn_rows = bn.rearrange("v j g o -> (v j g) o")
+        b_rows = b.rearrange("v g o -> (v g) o")
+        dw_rows = dw.rearrange("i j g o -> (i j g) o")
         nc.scalar.dma_start(out=rows[:, 0, :], in_=bn_rows[0:P])
         nc.scalar.dma_start(out=rows[0:32, 1, :], in_=bn_rows[P : P + 32])
-        nc.scalar.dma_start(out=rows[32:72, 1, :], in_=b.rearrange("v g o -> (v g) o"))
-        nc.scalar.dma_start(out=rows[0:72, 2, :], in_=dw.rearrange("i j g o -> (i j g) o"))
+        nc.scalar.dma_start(out=rows[32:64, 1, :], in_=b_rows[0:32])
+        nc.scalar.dma_start(out=rows[64:72, 1, :], in_=b_rows[32:40])
+        nc.scalar.dma_start(out=rows[0:64, 2, :], in_=dw_rows[0:64])
+        nc.scalar.dma_start(out=rows[64:72, 2, :], in_=dw_rows[64:72])
 
         w_planes = keep.tile([P, NV * G, P], U8, align_bytes=64)
         nc.vector.memset(w_planes[:].bitcast(I32), 0)
@@ -83,20 +88,25 @@ def tile_timeception_pa_e_kernel(tc, x, w_words, w_scales, b, dw, bn, out):
                 in_=words_dram[mats].rearrange("e p c -> p e c"),
             )
 
-        x_rows = x.rearrange("n t p q c -> n (t p q) c")
-        x_sb = [keep.tile([P, G * K], BF16, name="x_sb%d" % n) for n in range(NB)]
+        x_rows = x.rearrange("n t p q c -> (t p q) n c")
+        x_sb = {}
 
         def load_x(first_group, last_group):
-            cols = slice(K * first_group, K * (last_group + 1))
-            for n in range(NB):
-                nc.sync.dma_start(out=x_sb[n][:, cols], in_=x_rows[n, :, cols])
+            count = last_group + 1 - first_group
+            piece = keep.tile([P, NB, K * count], BF16, name="x_sb%d" % first_group)
+            nc.sync.dma_start(
+                out=piece[:], in_=x_rows[:, :, K * first_group : K * (last_group + 1)]
+            )
+            for g in range(first_group, last_group + 1):
+                x_sb[g] = (piece, g - first_group)
 
         load_x(0, 0)
+        load_x(1, 1)
+        load_x(2, 3)
         load_scales(3, 4)
         load_words(3, 3)
-        load_x(1, 1)
-        for pair in range(1, PAIRS):
-            load_x(2 * pair, 2 * pair + 1)
+        load_x(4, 5)
+        load_x(6, 7)
         load_scales(0, 2)
         load_words(4, 4)
         load_words(2, 2)
@@ -107,11 +117,16 @@ def tile_timeception_pa_e_kernel(tc, x, w_words, w_scales, b, dw, bn, out):
         ident = keep.tile([P, P], F32)
         make_identity(nc, ident[:])
 
-        nc.scalar.activation(out=one[:], in_=one[:], func=ACT.Sqrt)
+        nc.scalar.activation(out=one[:], in_=one[:], func=ACT.Abs_reciprocal_sqrt)
 
-        par_ps = psum_t.tile([P, 3, P], BF16, tag="xt")
+        par_ps = psum_o.tile([P, 3, P], BF16, tag="turned")
         for c in range(3):
             nc.tensor.transpose(par_ps[:, c, :], rows[:, c, :], ident_bf[:])
+        var_ps = par_ps[:].rearrange("p c r -> p (c r)")[:, 0 : NV * 4 * G].rearrange(
+            "p (v j g) -> p v j g", v=NV, j=4
+        )[:, :, 3, :]
+        inv_std = keep.tile([P, NV, G], F32)
+        nc.scalar.activation(out=inv_std[:], in_=var_ps, func=ACT.Abs_reciprocal_sqrt, bias=EPS, scale=1.0)
         par = keep.tile([P, 3 * P], F32)
         nc.vector.tensor_copy(out=par[:], in_=par_ps[:].rearrange("p c r -> p (c r)"))
 
@@ -119,55 +134,66 @@ def tile_timeception_pa_e_kernel(tc, x, w_words, w_scales, b, dw, bn, out):
         gamma = bn_par[:, :, 0, :]
         beta = bn_par[:, :, 1, :]
         mean = bn_par[:, :, 2, :]
-        var = bn_par[:, :, 3, :]
         bias = par[:, 160:200].rearrange("p (v g) -> p v g", v=NV)
         dw_par = par[:, 256:328].rearrange("p (i j g) -> p i j g", i=3, j=3)
 
-        scale = keep.tile([P, NV, G], F32)
-        nc.vector.tensor_scalar_add(out=scale[:], in0=var, scalar1=EPS)
-        nc.scalar.activation(out=scale[:], in_=scale[:], func=ACT.Sqrt)
-        nc.vector.reciprocal(out=scale[:], in_=scale[:])
-        nc.vector.tensor_mul(out=scale[:], in0=scale[:], in1=gamma)
-        shift = keep.tile([P, NV, G], F32)
-        nc.vector.tensor_mul(out=shift[:], in0=mean, in1=scale[:])
-        nc.vector.tensor_sub(out=shift[:], in0=beta, in1=shift[:])
+        tap_sum = keep.tile([P, NV, G], F32)
+        nc.vector.memset(tap_sum[:], 1.0)
+        nc.vector.tensor_reduce(
+            out=tap_sum[:, 1:4, :], in_=dw_par.rearrange("p i j g -> p i g j"),
+            axis=mybir.AxisListType.X, op=ALU.add,
+        )
         offset = keep.tile([P, NV, G], F32)
-        nc.vector.tensor_mul(out=offset[:], in0=bias, in1=scale[:])
-        nc.vector.tensor_add(out=offset[:], in0=offset[:], in1=shift[:])
+        nc.vector.tensor_mul(out=offset[:], in0=tap_sum[:], in1=bias)
+        nc.vector.tensor_sub(out=offset[:], in0=offset[:], in1=mean)
+        scale = keep.tile([P, NV, G], F32)
+        nc.vector.tensor_mul(out=scale[:], in0=inv_std[:], in1=gamma)
         spread = [P, 3, 3, G]
         taps = keep.tile(spread, F32)
         nc.vector.tensor_mul(
             out=taps[:], in0=dw_par, in1=scale[:, 1:4, :].unsqueeze(2).to_broadcast(spread)
         )
+        nc.vector.tensor_mul(out=offset[:], in0=offset[:], in1=scale[:])
+        nc.vector.tensor_add(out=offset[:], in0=offset[:], in1=beta)
         tap_bias = keep.tile(spread, F32)
         nc.vector.tensor_mul(
             out=tap_bias[:], in0=taps[:], in1=bias[:, 1:4, :].unsqueeze(2).to_broadcast(spread)
         )
-        conv_offset = keep.tile([P, 3, G], F32)
-        nc.vector.tensor_add(out=conv_offset[:], in0=tap_bias[:, :, 0, :], in1=tap_bias[:, :, 1, :])
-        nc.vector.tensor_add(out=conv_offset[:], in0=conv_offset[:], in1=tap_bias[:, :, 2, :])
-        nc.vector.tensor_add(out=conv_offset[:], in0=conv_offset[:], in1=shift[:, 1:4, :])
 
         x_codes = keep.tile([P, G, ROWS], U32, align_bytes=64)
         x_planes = keep.tile([P, G, ROWS], U8, align_bytes=64)
-        for g in range(G):
-            xt = psum_t.tile([P, 2, ROWS], F32, tag="xt")
-            for n in range(NB):
-                words = x_sb[n][:].bitcast(F32)
-                for u in range(2):
-                    nc.tensor.transpose(
-                        xt[:, u, COLS * n : COLS * (n + 1)],
-                        words[:, (K // 2) * g + u : (K // 2) * (g + 1) : 2],
-                        ident[:],
-                    )
-            grouped = stage.tile([P, ROWS * 4], BF16, align_bytes=64)
-            nc.scalar.copy(
-                out=grouped[:].bitcast(F32).rearrange("p (r u) -> p r u", u=2),
-                in_=xt[:].rearrange("p u r -> p r u"),
-            )
-            nc.vector.quantize_mx(
-                out=x_codes[:, g, :].bitcast(FP8X4), scales=x_planes[:, g, :], in_=grouped[:]
-            )
+        xt_tiles = {}
+        grouped_tiles = {}
+
+        def transpose_x(pair):
+            for g in (2 * pair, 2 * pair + 1):
+                xt = psum_t.tile([P, 2, ROWS], F32, tag="xt")
+                xt_tiles[g] = xt
+                piece, place = x_sb[g]
+                for n in range(NB):
+                    words = piece[:, n, :].bitcast(F32)
+                    for u in range(2):
+                        nc.tensor.transpose(
+                            xt[:, u, COLS * n : COLS * (n + 1)],
+                            words[:, (K // 2) * place + u : (K // 2) * (place + 1) : 2],
+                            ident[:],
+                        )
+
+        def regroup_x(pair):
+            for g in (2 * pair, 2 * pair + 1):
+                grouped = regrouped.tile([P, ROWS * 4], BF16, align_bytes=64)
+                grouped_tiles[g] = grouped
+                nc.scalar.copy(
+                    out=grouped[:].bitcast(F32).rearrange("p (r u) -> p r u", u=2),
+                    in_=xt_tiles[g][:].rearrange("p u r -> p r u"),
+                )
+
+        def quantise_x(pair):
+            for g in (2 * pair, 2 * pair + 1):
+                nc.vector.quantize_mx(
+                    out=x_codes[:, g, :].bitcast(FP8X4), scales=x_planes[:, g, :],
+                    in_=grouped_tiles[g][:],
+                )
 
         steps = work_order()
         y_tiles = {}
@@ -215,7 +241,7 @@ def tile_timeception_pa_e_kernel(tc, x, w_words, w_scales, b, dw, bn, out):
                 else:
                     nc.scalar.activation(
                         out=zg, in_=yg, func=ACT.Identity,
-                        scale=taps[:, v - 1, 1, g : g + 1], bias=conv_offset[:, v - 1, g : g + 1],
+                        scale=taps[:, v - 1, 1, g : g + 1], bias=offset[:, v, g : g + 1],
                     )
 
         def add_tap(j, tap):
@@ -281,7 +307,7 @@ def tile_timeception_pa_e_kernel(tc, x, w_words, w_scales, b, dw, bn, out):
             )
 
         def turn(v, h):
-            turned = psum_o.tile([P, HALF, P], F32)
+            turned = psum_o.tile([P, HALF, P], F32, tag="turned")
             turned_tiles[v, h] = turned
             for i in range(HALF):
                 nc.tensor.transpose(turned[:, i, :], pooled_tiles[v, h][:, i, :], ident[:])
@@ -303,7 +329,7 @@ def tile_timeception_pa_e_kernel(tc, x, w_words, w_scales, b, dw, bn, out):
                 )
 
         with tc.manual_schedule():
-            for j in range(-2, len(steps) + 5):
+            for j in range(-4, len(steps) + 5):
                 now = steps[j] if 0 <= j < len(steps) else None
                 if now is not None and now[0] in CONV:
                     add_tap(j, 0)
@@ -315,14 +341,20 @@ def tile_timeception_pa_e_kernel(tc, x, w_words, w_scales, b, dw, bn, out):
                     pool_pairs(*finished(j - 2))
                 if now is not None and now[0] in CONV:
                     add_tap(j, 2)
+                if 0 <= j + 2 < PAIRS:
+                    quantise_x(j + 2)
 
                 if 0 <= j + 2 < len(steps):
                     multiply(j + 2)
                 if finished(j - 3) is not None:
                     turn(*finished(j - 3))
+                if 0 <= j + 4 < PAIRS:
+                    transpose_x(j + 4)
 
                 if 0 <= j + 1 < len(steps):
                     leave_psum(j + 1)
+                if 0 <= j + 3 < PAIRS:
+                    regroup_x(j + 3)
                 if now is not None and now[0] == 4:
                     normalise(j)
                 if finished(j - 4) is not None:

@@ -60,12 +60,16 @@ def tile_timeception_pa_e_kernel(tc, x, w_words, w_scales, b, dw, bn, out):
         bn_rows = bn.rearrange("v j g o -> (v j g) o")
         b_rows = b.rearrange("v g o -> (v g) o")
         dw_rows = dw.rearrange("i j g o -> (i j g) o")
-        nc.scalar.dma_start(out=rows[:, 0, :], in_=bn_rows[0:P])
-        nc.scalar.dma_start(out=rows[0:32, 1, :], in_=bn_rows[P : P + 32])
-        nc.scalar.dma_start(out=rows[32:64, 1, :], in_=b_rows[0:32])
-        nc.scalar.dma_start(out=rows[64:72, 1, :], in_=b_rows[32:40])
-        nc.scalar.dma_start(out=rows[0:64, 2, :], in_=dw_rows[0:64])
-        nc.scalar.dma_start(out=rows[64:72, 2, :], in_=dw_rows[64:72])
+
+        def load_parameters():
+            nc.sync.dma_start(out=rows[:, 0, :], in_=bn_rows[0:P])
+            nc.sync.dma_start(out=rows[0:32, 1, :], in_=bn_rows[P : P + 32])
+            nc.sync.dma_start(out=rows[32:64, 1, :], in_=b_rows[0:32])
+            nc.sync.dma_start(out=rows[64:72, 1, :], in_=b_rows[32:40])
+            nc.sync.dma_start(out=rows[0:64, 2, :], in_=dw_rows[0:64])
+            nc.sync.dma_start(out=rows[64:72, 2, :], in_=dw_rows[64:72])
+
+        nc.scalar.activation(out=one[:], in_=one[:], func=ACT.Abs_reciprocal_sqrt)
 
         w_planes = keep.tile([P, NV * G, P], U8, align_bytes=64)
         nc.vector.memset(w_planes[:].bitcast(I32), 0)
@@ -102,6 +106,7 @@ def tile_timeception_pa_e_kernel(tc, x, w_words, w_scales, b, dw, bn, out):
 
         load_x(0, 0)
         load_x(1, 1)
+        load_parameters()
         load_x(2, 3)
         load_scales(3, 4)
         load_words(3, 3)
@@ -117,83 +122,86 @@ def tile_timeception_pa_e_kernel(tc, x, w_words, w_scales, b, dw, bn, out):
         ident = keep.tile([P, P], F32)
         make_identity(nc, ident[:])
 
-        nc.scalar.activation(out=one[:], in_=one[:], func=ACT.Abs_reciprocal_sqrt)
-
         par_ps = psum_o.tile([P, 3, P], BF16, tag="turned")
-        for c in range(3):
-            nc.tensor.transpose(par_ps[:, c, :], rows[:, c, :], ident_bf[:])
-        var_ps = par_ps[:].rearrange("p c r -> p (c r)")[:, 0 : NV * 4 * G].rearrange(
-            "p (v j g) -> p v j g", v=NV, j=4
-        )[:, :, 3, :]
-        inv_std = keep.tile([P, NV, G], F32)
-        nc.scalar.activation(out=inv_std[:], in_=var_ps, func=ACT.Abs_reciprocal_sqrt, bias=EPS, scale=1.0)
-        par = keep.tile([P, 3 * P], F32)
-        nc.vector.tensor_copy(out=par[:], in_=par_ps[:].rearrange("p c r -> p (c r)"))
-
+        par = par_ps[:].rearrange("p c r -> p (c r)")
         bn_par = par[:, 0 : NV * 4 * G].rearrange("p (v j g) -> p v j g", v=NV, j=4)
         gamma = bn_par[:, :, 0, :]
         beta = bn_par[:, :, 1, :]
         mean = bn_par[:, :, 2, :]
+        var = bn_par[:, :, 3, :]
         bias = par[:, 160:200].rearrange("p (v g) -> p v g", v=NV)
         dw_par = par[:, 256:328].rearrange("p (i j g) -> p i j g", i=3, j=3)
 
+        inv_std = keep.tile([P, NV, G], F32)
         tap_sum = keep.tile([P, NV, G], F32)
         nc.vector.memset(tap_sum[:], 1.0)
-        nc.vector.tensor_reduce(
-            out=tap_sum[:, 1:4, :], in_=dw_par.rearrange("p i j g -> p i g j"),
-            axis=mybir.AxisListType.X, op=ALU.add,
-        )
         offset = keep.tile([P, NV, G], F32)
-        nc.vector.tensor_mul(out=offset[:], in0=tap_sum[:], in1=bias)
-        nc.vector.tensor_sub(out=offset[:], in0=offset[:], in1=mean)
         scale = keep.tile([P, NV, G], F32)
-        nc.vector.tensor_mul(out=scale[:], in0=inv_std[:], in1=gamma)
         spread = [P, 3, 3, G]
         taps = keep.tile(spread, F32)
-        nc.vector.tensor_mul(
-            out=taps[:], in0=dw_par, in1=scale[:, 1:4, :].unsqueeze(2).to_broadcast(spread)
-        )
-        nc.vector.tensor_mul(out=offset[:], in0=offset[:], in1=scale[:])
-        nc.vector.tensor_add(out=offset[:], in0=offset[:], in1=beta)
         tap_bias = keep.tile(spread, F32)
-        nc.vector.tensor_mul(
-            out=tap_bias[:], in0=taps[:], in1=bias[:, 1:4, :].unsqueeze(2).to_broadcast(spread)
-        )
+
+        def transpose_parameters():
+            for c in range(3):
+                nc.tensor.transpose(par_ps[:, c, :], rows[:, c, :], ident_bf[:])
+
+        def invert_std():
+            nc.scalar.activation(
+                out=inv_std[:], in_=var, func=ACT.Abs_reciprocal_sqrt, bias=EPS, scale=1.0
+            )
+
+        def before_scale():
+            nc.vector.tensor_reduce(
+                out=tap_sum[:, 1:4, :], in_=dw_par.rearrange("p i j g -> p i g j"),
+                axis=mybir.AxisListType.X, op=ALU.add,
+            )
+            nc.vector.tensor_mul(out=offset[:], in0=tap_sum[:], in1=bias)
+            nc.vector.tensor_sub(out=offset[:], in0=offset[:], in1=mean)
+
+        def after_scale():
+            nc.vector.tensor_mul(out=scale[:], in0=inv_std[:], in1=gamma)
+            nc.vector.tensor_mul(
+                out=taps[:], in0=dw_par, in1=scale[:, 1:4, :].unsqueeze(2).to_broadcast(spread)
+            )
+            nc.vector.tensor_mul(out=offset[:], in0=offset[:], in1=scale[:])
+            nc.vector.tensor_add(out=offset[:], in0=offset[:], in1=beta)
+
+        def edge_terms():
+            nc.vector.tensor_mul(
+                out=tap_bias[:], in0=taps[:], in1=bias[:, 1:4, :].unsqueeze(2).to_broadcast(spread)
+            )
 
         x_codes = keep.tile([P, G, ROWS], U32, align_bytes=64)
         x_planes = keep.tile([P, G, ROWS], U8, align_bytes=64)
         xt_tiles = {}
         grouped_tiles = {}
 
-        def transpose_x(pair):
-            for g in (2 * pair, 2 * pair + 1):
-                xt = psum_t.tile([P, 2, ROWS], F32, tag="xt")
-                xt_tiles[g] = xt
-                piece, place = x_sb[g]
-                for n in range(NB):
-                    words = piece[:, n, :].bitcast(F32)
-                    for u in range(2):
-                        nc.tensor.transpose(
-                            xt[:, u, COLS * n : COLS * (n + 1)],
-                            words[:, (K // 2) * place + u : (K // 2) * (place + 1) : 2],
-                            ident[:],
-                        )
+        def transpose_x(g):
+            xt = psum_t.tile([P, 2, ROWS], F32, tag="xt")
+            xt_tiles[g] = xt
+            piece, place = x_sb[g]
+            for n in range(NB):
+                words = piece[:, n, :].bitcast(F32)
+                for u in range(2):
+                    nc.tensor.transpose(
+                        xt[:, u, COLS * n : COLS * (n + 1)],
+                        words[:, (K // 2) * place + u : (K // 2) * (place + 1) : 2],
+                        ident[:],
+                    )
 
-        def regroup_x(pair):
-            for g in (2 * pair, 2 * pair + 1):
-                grouped = regrouped.tile([P, ROWS * 4], BF16, align_bytes=64)
-                grouped_tiles[g] = grouped
-                nc.scalar.copy(
-                    out=grouped[:].bitcast(F32).rearrange("p (r u) -> p r u", u=2),
-                    in_=xt_tiles[g][:].rearrange("p u r -> p r u"),
-                )
+        def regroup_x(g):
+            grouped = regrouped.tile([P, ROWS * 4], BF16, align_bytes=64)
+            grouped_tiles[g] = grouped
+            nc.scalar.copy(
+                out=grouped[:].bitcast(F32).rearrange("p (r u) -> p r u", u=2),
+                in_=xt_tiles[g][:].rearrange("p u r -> p r u"),
+            )
 
-        def quantise_x(pair):
-            for g in (2 * pair, 2 * pair + 1):
-                nc.vector.quantize_mx(
-                    out=x_codes[:, g, :].bitcast(FP8X4), scales=x_planes[:, g, :],
-                    in_=grouped_tiles[g][:],
-                )
+        def quantise_x(g):
+            nc.vector.quantize_mx(
+                out=x_codes[:, g, :].bitcast(FP8X4), scales=x_planes[:, g, :],
+                in_=grouped_tiles[g][:],
+            )
 
         steps = work_order()
         y_tiles = {}
@@ -329,7 +337,18 @@ def tile_timeception_pa_e_kernel(tc, x, w_words, w_scales, b, dw, bn, out):
                 )
 
         with tc.manual_schedule():
-            for j in range(-4, len(steps) + 5):
+            transpose_x(0)
+            transpose_parameters()
+            transpose_x(1)
+            regroup_x(0)
+            invert_std()
+            regroup_x(1)
+            before_scale()
+            quantise_x(0)
+            after_scale()
+            quantise_x(1)
+            edge_terms()
+            for j in range(-3, len(steps) + 5):
                 now = steps[j] if 0 <= j < len(steps) else None
                 if now is not None and now[0] in CONV:
                     add_tap(j, 0)
@@ -341,20 +360,23 @@ def tile_timeception_pa_e_kernel(tc, x, w_words, w_scales, b, dw, bn, out):
                     pool_pairs(*finished(j - 2))
                 if now is not None and now[0] in CONV:
                     add_tap(j, 2)
-                if 0 <= j + 2 < PAIRS:
-                    quantise_x(j + 2)
+                if 1 <= j + 2 < PAIRS:
+                    quantise_x(2 * (j + 2))
+                    quantise_x(2 * (j + 2) + 1)
 
                 if 0 <= j + 2 < len(steps):
                     multiply(j + 2)
                 if finished(j - 3) is not None:
                     turn(*finished(j - 3))
-                if 0 <= j + 4 < PAIRS:
-                    transpose_x(j + 4)
+                if 1 <= j + 4 < PAIRS:
+                    transpose_x(2 * (j + 4))
+                    transpose_x(2 * (j + 4) + 1)
 
                 if 0 <= j + 1 < len(steps):
                     leave_psum(j + 1)
-                if 0 <= j + 3 < PAIRS:
-                    regroup_x(j + 3)
+                if 1 <= j + 3 < PAIRS:
+                    regroup_x(2 * (j + 3))
+                    regroup_x(2 * (j + 3) + 1)
                 if now is not None and now[0] == 4:
                     normalise(j)
                 if finished(j - 4) is not None:

@@ -279,10 +279,9 @@ def tile_timeception_pa_e_kernel(tc, x, w_words, w_scales, b, dw, bn, out):
         def normalise(j):
             v, pair = steps[j]
             for g in (2 * pair, 2 * pair + 1):
-                nc.gpsimd.tensor_scalar(
-                    out=z_tiles[v][:, g, :], in0=z_tiles[v][:, g, :],
-                    scalar1=scale[:, v, g : g + 1], scalar2=offset[:, v, g : g + 1],
-                    op0=ALU.mult, op1=ALU.add,
+                nc.scalar.activation(
+                    out=z_tiles[v][:, g, :], in_=z_tiles[v][:, g, :], func=ACT.Identity,
+                    scale=scale[:, v, g : g + 1], bias=offset[:, v, g : g + 1],
                 )
 
         def finished(j):
@@ -377,7 +376,7 @@ def tile_timeception_pa_e_kernel(tc, x, w_words, w_scales, b, dw, bn, out):
                 if 1 <= j + 3 < PAIRS:
                     regroup_x(2 * (j + 3))
                     regroup_x(2 * (j + 3) + 1)
-                if now is not None and now[0] == 4:
-                    normalise(j)
+                if 0 <= j - 1 < len(steps) and steps[j - 1][0] == 4:
+                    normalise(j - 1)
                 if finished(j - 4) is not None:
                     shuffle_out(*finished(j - 4))

@@ -21,6 +21,7 @@ G = 8
 K = 512
 NV = 5
 EPS = 1e-3
+FAR = 3.0e38
 COLS = T * S
 ROWS = NB * COLS
 PAIRS = G // 2
@@ -49,6 +50,7 @@ def tile_timeception_pa_e_kernel(tc, x, w_words, w_scales, b, dw, bn, out):
         stage = ctx.enter_context(tc.tile_pool(name="stage", bufs=2))
         branch = ctx.enter_context(tc.tile_pool(name="branch", bufs=4))
         regrouped = ctx.enter_context(tc.tile_pool(name="regrouped", bufs=4))
+        fourth = ctx.enter_context(tc.tile_pool(name="fourth", bufs=2))
         psum_t = ctx.enter_context(tc.psum_pool(name="psum_t", bufs=2))
         psum_y = ctx.enter_context(tc.psum_pool(name="psum_y", bufs=4))
         psum_o = ctx.enter_context(tc.psum_pool(name="psum_o", bufs=2))
@@ -166,9 +168,22 @@ def tile_timeception_pa_e_kernel(tc, x, w_words, w_scales, b, dw, bn, out):
             nc.vector.tensor_mul(out=offset[:], in0=offset[:], in1=scale[:])
             nc.vector.tensor_add(out=offset[:], in0=offset[:], in1=beta)
 
+        sign = keep.tile([P, G], F32)
+        even = keep.tile([P, G, NB, T // 2 + 1, S], F32)
+
         def edge_terms():
             nc.vector.tensor_mul(
                 out=tap_bias[:], in0=taps[:], in1=bias[:, 1:4, :].unsqueeze(2).to_broadcast(spread)
+            )
+            nc.vector.tensor_scalar(
+                out=sign[:], in0=scale[:, 4, :], scalar1=0.0, scalar2=2.0,
+                op0=ALU.is_ge, op1=ALU.mult,
+            )
+            nc.vector.tensor_scalar_add(out=sign[:], in0=sign[:], scalar1=-1.0)
+            nc.vector.tensor_scalar_mul(
+                out=even[:, :, :, T // 2, :],
+                in0=sign[:].unsqueeze(2).unsqueeze(3).to_broadcast([P, G, NB, S]),
+                scalar1=-FAR,
             )
 
         x_codes = keep.tile([P, G, ROWS], U32, align_bytes=64)
@@ -213,6 +228,9 @@ def tile_timeception_pa_e_kernel(tc, x, w_words, w_scales, b, dw, bn, out):
         def by_batch(ap):
             return ap.rearrange("p (n c) -> p n c", n=NB)
 
+        def by_parity(ap, odd):
+            return ap.rearrange("p (n m two s) -> p n m two s", n=NB, two=2, s=S)[:, :, :, odd, :]
+
         def multiply(j):
             v, pair = steps[j]
             y = psum_y.tile([P, 2, ROWS], F32)
@@ -231,12 +249,17 @@ def tile_timeception_pa_e_kernel(tc, x, w_words, w_scales, b, dw, bn, out):
 
         def leave_psum(j):
             v, pair = steps[j]
+            if v == 4:
+                for i in range(2):
+                    g = 2 * pair + i
+                    nc.scalar.activation(
+                        out=even[:, g, :, 0 : T // 2, :], in_=by_parity(y_tiles[j][:, i, :], 0),
+                        func=ACT.Copy, scale=sign[:, g : g + 1],
+                    )
+                return
             if pair == 0:
                 z = branch.tile([P, G, ROWS], F32)
                 z_tiles[v] = z
-            if v == 4:
-                nc.scalar.copy(out=z_tiles[v][:, 2 * pair : 2 * pair + 2, :], in_=y_tiles[j][:])
-                return
             for i in range(2):
                 g = 2 * pair + i
                 zg = z_tiles[v][:, g, :]
@@ -268,19 +291,40 @@ def tile_timeception_pa_e_kernel(tc, x, w_words, w_scales, b, dw, bn, out):
                     op0=ALU.mult, op1=ALU.add,
                 )
 
-        def max_with_next(j):
+        window_tiles = {}
+
+        def widen(j):
             v, pair = steps[j]
-            z_nt = z_tiles[v][:, 2 * pair : 2 * pair + 2, :].rearrange("p g (n c) -> p (g n) c", n=NB)
-            y_nt = y_tiles[j][:].rearrange("p g (n c) -> p (g n) c", n=NB)
-            nc.vector.tensor_max(
-                out=z_nt[:, :, : COLS - S], in0=z_nt[:, :, : COLS - S], in1=y_nt[:, :, S:]
-            )
+            window = fourth.tile([P, 2, NB, T // 2, S], F32)
+            window_tiles[j] = window
+            for i in range(2):
+                g = 2 * pair + i
+                nc.vector.tensor_max(
+                    out=window[:, i], in0=even[:, g, :, 0 : T // 2, :], in1=even[:, g, :, 1 : T // 2 + 1, :]
+                )
+
+        def choose(j):
+            v, pair = steps[j]
+            if pair % 2 == 0:
+                chosen = fourth.tile([P, HALF, COLS], F32)
+                pooled_tiles[v, pair // 2] = chosen
+            for i in range(2):
+                g = 2 * pair + i
+                nc.vector.scalar_tensor_tensor(
+                    out=pooled_tiles[v, pair // 2][:, g % HALF, :].rearrange(
+                        "p (n m s) -> p n m s", n=NB, s=S
+                    ),
+                    in0=window_tiles[j][:, i], scalar=sign[:, g : g + 1],
+                    in1=by_parity(y_tiles[j][:, i, :], 1),
+                    op0=ALU.mult, op1=ALU.max,
+                )
 
         def normalise(j):
             v, pair = steps[j]
             for g in (2 * pair, 2 * pair + 1):
+                chosen_g = pooled_tiles[v, pair // 2][:, g % HALF, :]
                 nc.scalar.activation(
-                    out=z_tiles[v][:, g, :], in_=z_tiles[v][:, g, :], func=ACT.Identity,
+                    out=chosen_g, in_=chosen_g, func=ACT.Relu,
                     scale=scale[:, v, g : g + 1], bias=offset[:, v, g : g + 1],
                 )
 
@@ -352,13 +396,15 @@ def tile_timeception_pa_e_kernel(tc, x, w_words, w_scales, b, dw, bn, out):
                 if now is not None and now[0] in CONV:
                     add_tap(j, 0)
                 if now is not None and now[0] == 4:
-                    max_with_next(j)
+                    widen(j)
                 if finished(j - 1) is not None and finished(j - 1)[0] in CONV:
                     mend_edges(*finished(j - 1))
-                if finished(j - 2) is not None:
+                if finished(j - 2) is not None and finished(j - 2)[0] != 4:
                     pool_pairs(*finished(j - 2))
                 if now is not None and now[0] in CONV:
                     add_tap(j, 2)
+                if now is not None and now[0] == 4:
+                    choose(j)
                 if 1 <= j + 2 < PAIRS:
                     quantise_x(2 * (j + 2))
                     quantise_x(2 * (j + 2) + 1)

from contextlib import ExitStack

import concourse.mybir as mybir
from concourse.masks import make_identity

F32 = mybir.dt.float32
BF16 = mybir.dt.bfloat16
I32 = mybir.dt.int32
U32 = mybir.dt.uint32
U8 = mybir.dt.uint8
FP8X4 = mybir.dt.float8_e4m3fn_x4
FP4X4 = mybir.dt.float4_e2m1fn_x4
ALU = mybir.AluOpType
ACT = mybir.ActivationFunctionType

P = 128
NB = 2
T = 32
S = 4
G = 8
K = 512
NV = 5
EPS = 1e-3
FAR = 3.0e38
COLS = T * S
ROWS = NB * COLS
PAIRS = G // 2
HALF = G // 2

CONV = (3, 2, 1)
OTHER = (4, 0)

FLOPS = 2 * ROWS * K * P * NV * G


def work_order():
    conv = [(v, pair) for v in CONV for pair in range(PAIRS)]
    other = [(v, pair) for v in OTHER for pair in range(PAIRS)]
    steps = conv[:PAIRS]
    for i in range(len(other)):
        steps.append(other[i])
        steps.append(conv[PAIRS + i])
    return steps


def tile_timeception_pa_e_kernel(tc, x, w_words, w_scales, b, dw, bn, out):
    nc = tc.nc
    with ExitStack() as ctx:
        keep = ctx.enter_context(tc.tile_pool(name="keep", bufs=1))
        stage = ctx.enter_context(tc.tile_pool(name="stage", bufs=2))
        branch = ctx.enter_context(tc.tile_pool(name="branch", bufs=4))
        regrouped = ctx.enter_context(tc.tile_pool(name="regrouped", bufs=4))
        fourth = ctx.enter_context(tc.tile_pool(name="fourth", bufs=2))
        psum_t = ctx.enter_context(tc.psum_pool(name="psum_t", bufs=2))
        psum_y = ctx.enter_context(tc.psum_pool(name="psum_y", bufs=4))
        psum_o = ctx.enter_context(tc.psum_pool(name="psum_o", bufs=2))

        one = keep.tile([P, 1], F32)
        nc.vector.memset(one[:], 1.0)
        rows = keep.tile([P, 3, P], BF16)
        nc.vector.memset(rows[:, 1:3, :], 0.0)
        bn_rows = bn.rearrange("v j g o -> (v j g) o")
        b_rows = b.rearrange("v g o -> (v g) o")
        dw_rows = dw.rearrange("i j g o -> (i j g) o")

        def load_parameters():
            nc.sync.dma_start(out=rows[:, 0, :], in_=bn_rows[0:P])
            nc.sync.dma_start(out=rows[0:32, 1, :], in_=bn_rows[P : P + 32])
            nc.sync.dma_start(out=rows[32:64, 1, :], in_=b_rows[0:32])
            nc.sync.dma_start(out=rows[64:72, 1, :], in_=b_rows[32:40])
            nc.sync.dma_start(out=rows[0:64, 2, :], in_=dw_rows[0:64])
            nc.sync.dma_start(out=rows[64:72, 2, :], in_=dw_rows[64:72])

        nc.scalar.activation(out=one[:], in_=one[:], func=ACT.Abs_reciprocal_sqrt)

        w_planes = keep.tile([P, NV * G, P], U8, align_bytes=64)
        nc.vector.memset(w_planes[:].bitcast(I32), 0)
        w_sb = keep.tile([P, NV * G, 2 * P], U8, align_bytes=64)
        words_dram = w_words.bitcast(I32)
        scales_dram = w_scales.bitcast(I32)

        def load_scales(first_branch, last_branch):
            mats = slice(G * first_branch, G * (last_branch + 1))
            for r in range(4):
                nc.sync.dma_start(
                    out=w_planes[r:P:32, mats, :].bitcast(I32),
                    in_=scales_dram[mats, r:16:4, :].rearrange("e q c -> q e c"),
                )

        def load_words(first_branch, last_branch):
            mats = slice(G * first_branch, G * (last_branch + 1))
            nc.sync.dma_start(
                out=w_sb[:, mats, :].bitcast(I32),
                in_=words_dram[mats].rearrange("e p c -> p e c"),
            )

        x_rows = x.rearrange("n t p q c -> (t p q) n c")
        x_sb = {}

        def load_x(first_group, last_group):
            count = last_group + 1 - first_group
            piece = keep.tile([P, NB, K * count], BF16, name="x_sb%d" % first_group)
            nc.sync.dma_start(
                out=piece[:], in_=x_rows[:, :, K * first_group : K * (last_group + 1)]
            )
            for g in range(first_group, last_group + 1):
                x_sb[g] = (piece, g - first_group)

        load_x(0, 0)
        load_x(1, 1)
        load_parameters()
        load_x(2, 3)
        load_scales(3, 4)
        load_words(3, 3)
        load_x(4, 5)
        load_x(6, 7)
        load_scales(0, 2)
        load_words(4, 4)
        load_words(2, 2)
        load_words(0, 1)

        ident_bf = keep.tile([P, P], BF16)
        make_identity(nc, ident_bf[:])
        ident = keep.tile([P, P], F32)
        make_identity(nc, ident[:])

        par_ps = psum_o.tile([P, 3, P], BF16, tag="turned")
        par = par_ps[:].rearrange("p c r -> p (c r)")
        bn_par = par[:, 0 : NV * 4 * G].rearrange("p (v j g) -> p v j g", v=NV, j=4)
        gamma = bn_par[:, :, 0, :]
        beta = bn_par[:, :, 1, :]
        mean = bn_par[:, :, 2, :]
        var = bn_par[:, :, 3, :]
        bias = par[:, 160:200].rearrange("p (v g) -> p v g", v=NV)
        dw_par = par[:, 256:328].rearrange("p (i j g) -> p i j g", i=3, j=3)

        inv_std = keep.tile([P, NV, G], F32)
        tap_sum = keep.tile([P, NV, G], F32)
        nc.vector.memset(tap_sum[:], 1.0)
        offset = keep.tile([P, NV, G], F32)
        scale = keep.tile([P, NV, G], F32)
        spread = [P, 3, 3, G]
        taps = keep.tile(spread, F32)
        tap_bias = keep.tile(spread, F32)

        def transpose_parameters():
            for c in range(3):
                nc.tensor.transpose(par_ps[:, c, :], rows[:, c, :], ident_bf[:])

        def invert_std():
            nc.scalar.activation(
                out=inv_std[:], in_=var, func=ACT.Abs_reciprocal_sqrt, bias=EPS, scale=1.0
            )

        def before_scale():
            nc.vector.tensor_reduce(
                out=tap_sum[:, 1:4, :], in_=dw_par.rearrange("p i j g -> p i g j"),
                axis=mybir.AxisListType.X, op=ALU.add,
            )
            nc.vector.tensor_mul(out=offset[:], in0=tap_sum[:], in1=bias)
            nc.vector.tensor_sub(out=offset[:], in0=offset[:], in1=mean)

        def after_scale():
            nc.vector.tensor_mul(out=scale[:], in0=inv_std[:], in1=gamma)
            nc.vector.tensor_mul(
                out=taps[:], in0=dw_par, in1=scale[:, 1:4, :].unsqueeze(2).to_broadcast(spread)
            )
            nc.vector.tensor_mul(out=offset[:], in0=offset[:], in1=scale[:])
            nc.vector.tensor_add(out=offset[:], in0=offset[:], in1=beta)

        sign = keep.tile([P, G], F32)
        even = keep.tile([P, G, NB, T // 2 + 1, S], F32)

        def edge_terms():
            nc.vector.tensor_mul(
                out=tap_bias[:], in0=taps[:], in1=bias[:, 1:4, :].unsqueeze(2).to_broadcast(spread)
            )
            nc.vector.tensor_scalar(
                out=sign[:], in0=scale[:, 4, :], scalar1=0.0, scalar2=2.0,
                op0=ALU.is_ge, op1=ALU.mult,
            )
            nc.vector.tensor_scalar_add(out=sign[:], in0=sign[:], scalar1=-1.0)
            nc.vector.tensor_scalar_mul(
                out=even[:, :, :, T // 2, :],
                in0=sign[:].unsqueeze(2).unsqueeze(3).to_broadcast([P, G, NB, S]),
                scalar1=-FAR,
            )

        x_codes = keep.tile([P, G, ROWS], U32, align_bytes=64)
        x_planes = keep.tile([P, G, ROWS], U8, align_bytes=64)
        xt_tiles = {}
        grouped_tiles = {}

        def transpose_x(g):
            xt = psum_t.tile([P, 2, ROWS], F32, tag="xt")
            xt_tiles[g] = xt
            piece, place = x_sb[g]
            for n in range(NB):
                words = piece[:, n, :].bitcast(F32)
                for u in range(2):
                    nc.tensor.transpose(
                        xt[:, u, COLS * n : COLS * (n + 1)],
                        words[:, (K // 2) * place + u : (K // 2) * (place + 1) : 2],
                        ident[:],
                    )

        def regroup_x(g):
            grouped = regrouped.tile([P, ROWS * 4], BF16, align_bytes=64)
            grouped_tiles[g] = grouped
            nc.scalar.copy(
                out=grouped[:].bitcast(F32).rearrange("p (r u) -> p r u", u=2),
                in_=xt_tiles[g][:].rearrange("p u r -> p r u"),
            )

        def quantise_x(g):
            nc.vector.quantize_mx(
                out=x_codes[:, g, :].bitcast(FP8X4), scales=x_planes[:, g, :],
                in_=grouped_tiles[g][:],
            )

        steps = work_order()
        y_tiles = {}
        z_tiles = {}
        results = {}
        pooled_tiles = {}
        turned_tiles = {}

        def by_batch(ap):
            return ap.rearrange("p (n c) -> p n c", n=NB)

        def by_parity(ap, odd):
            return ap.rearrange("p (n m two s) -> p n m two s", n=NB, two=2, s=S)[:, :, :, odd, :]

        def multiply(j):
            v, pair = steps[j]
            y = psum_y.tile([P, 2, ROWS], F32)
            y_tiles[j] = y
            for i in range(2):
                g = 2 * pair + i
                nc.tensor.matmul_mx(
                    out=y[:, i, :],
                    lhsT=w_sb[:, G * v + g, :].bitcast(FP4X4),
                    lhsT_scale=w_planes[:, G * v + g, :],
                    rhs=x_codes[:, g, :].bitcast(FP8X4),
                    rhs_scale=x_planes[:, g, :],
                    start=True,
                    stop=True,
                )

        def leave_psum(j):
            v, pair = steps[j]
            if v == 4:
                for i in range(2):
                    g = 2 * pair + i
                    nc.scalar.activation(
                        out=even[:, g, :, 0 : T // 2, :], in_=by_parity(y_tiles[j][:, i, :], 0),
                        func=ACT.Copy, scale=sign[:, g : g + 1],
                    )
                return
            if pair == 0:
                z = branch.tile([P, G, ROWS], F32)
                z_tiles[v] = z
            for i in range(2):
                g = 2 * pair + i
                zg = z_tiles[v][:, g, :]
                yg = y_tiles[j][:, i, :]
                if v == 0:
                    nc.scalar.activation(
                        out=zg, in_=yg, func=ACT.Identity,
                        scale=scale[:, v, g : g + 1], bias=offset[:, v, g : g + 1],
                    )
                else:
                    nc.scalar.activation(
                        out=zg, in_=yg, func=ACT.Identity,
                        scale=taps[:, v - 1, 1, g : g + 1], bias=offset[:, v, g : g + 1],
                    )

        def add_tap(j, tap):
            v, pair = steps[j]
            w = v * S
            for i in range(2):
                g = 2 * pair + i
                z_nt = by_batch(z_tiles[v][:, g, :])
                y_nt = by_batch(y_tiles[j][:, i, :])
                if tap == 0:
                    target, source = z_nt[:, :, w:], y_nt[:, :, : COLS - w]
                else:
                    target, source = z_nt[:, :, : COLS - w], y_nt[:, :, w:]
                nc.vector.scalar_tensor_tensor(
                    out=target, in0=source, scalar=taps[:, v - 1, tap, g : g + 1], in1=target,
                    op0=ALU.mult, op1=ALU.add,
                )

        window_tiles = {}

        def widen(j):
            v, pair = steps[j]
            window = fourth.tile([P, 2, NB, T // 2, S], F32)
            window_tiles[j] = window
            for i in range(2):
                g = 2 * pair + i
                nc.vector.tensor_max(
                    out=window[:, i], in0=even[:, g, :, 0 : T // 2, :], in1=even[:, g, :, 1 : T // 2 + 1, :]
                )

        def choose(j):
            v, pair = steps[j]
            if pair % 2 == 0:
                chosen = fourth.tile([P, HALF, COLS], F32)
                pooled_tiles[v, pair // 2] = chosen
            for i in range(2):
                g = 2 * pair + i
                nc.vector.scalar_tensor_tensor(
                    out=pooled_tiles[v, pair // 2][:, g % HALF, :].rearrange(
                        "p (n m s) -> p n m s", n=NB, s=S
                    ),
                    in0=window_tiles[j][:, i], scalar=sign[:, g : g + 1],
                    in1=by_parity(y_tiles[j][:, i, :], 1),
                    op0=ALU.mult, op1=ALU.max,
                )

        def normalise(j):
            v, pair = steps[j]
            for g in (2 * pair, 2 * pair + 1):
                chosen_g = pooled_tiles[v, pair // 2][:, g % HALF, :]
                nc.scalar.activation(
                    out=chosen_g, in_=chosen_g, func=ACT.Relu,
                    scale=scale[:, v, g : g + 1], bias=offset[:, v, g : g + 1],
                )

        def finished(j):
            if 0 <= j < len(steps) and steps[j][1] % 2 == 1:
                return steps[j][0], steps[j][1] // 2
            return None

        def mend_edges(v, h):
            groups = slice(HALF * h, HALF * (h + 1))
            w = v * S
            z_edges = z_tiles[v][:, groups, :].rearrange("p g (n c) -> p g n c", n=NB)
            for tap, cols in ((0, slice(0, w)), (2, slice(COLS - w, COLS))):
                extra = tap_bias[:, v - 1, tap, groups].unsqueeze(2).unsqueeze(3)
                nc.gpsimd.tensor_tensor(
                    out=z_edges[:, :, :, cols],
                    in0=z_edges[:, :, :, cols],
                    in1=extra.to_broadcast([P, HALF, NB, w]),
                    op=ALU.subtract,
                )

        def pool_pairs(v, h):
            groups = slice(HALF * h, HALF * (h + 1))
            pairs = z_tiles[v][:, groups, :].rearrange("p g (m two s) -> p (g m) two s", two=2, s=S)
            pooled = stage.tile([P, HALF, COLS], F32)
            pooled_tiles[v, h] = pooled
            nc.vector.scalar_tensor_tensor(
                out=pooled[:].rearrange("p g (m s) -> p (g m) s", s=S),
                in0=pairs[:, :, 0, :], scalar=0.0, in1=pairs[:, :, 1, :],
                op0=ALU.max, op1=ALU.max,
            )

        def turn(v, h):
            turned = psum_o.tile([P, HALF, P], F32, tag="turned")
            turned_tiles[v, h] = turned
            for i in range(HALF):
                nc.tensor.transpose(turned[:, i, :], pooled_tiles[v, h][:, i, :], ident[:])

        out_rows = out.rearrange("n t p q c -> (n t p q) c")

        def shuffle_out(v, h):
            if h == 0:
                result = branch.tile([P, P, G], F32)
                results[v] = result
            nc.scalar.copy(
                out=results[v][:, :, HALF * h : HALF * (h + 1)],
                in_=turned_tiles[v, h][:].rearrange("p g o -> p o g"),
            )
            if h == 1:
                nc.sync.dma_start(
                    out=out_rows[:, P * G * v : P * G * (v + 1)],
                    in_=results[v][:].rearrange("p o g -> p (o g)"),
                )

        with tc.manual_schedule():
            transpose_x(0)
            transpose_parameters()
            transpose_x(1)
            regroup_x(0)
            invert_std()
            regroup_x(1)
            before_scale()
            quantise_x(0)
            after_scale()
            quantise_x(1)
            edge_terms()
            for j in range(-3, len(steps) + 5):
                now = steps[j] if 0 <= j < len(steps) else None
                if now is not None and now[0] in CONV:
                    add_tap(j, 0)
                if now is not None and now[0] == 4:
                    widen(j)
                if finished(j - 1) is not None and finished(j - 1)[0] in CONV:
                    mend_edges(*finished(j - 1))
                if finished(j - 2) is not None and finished(j - 2)[0] != 4:
                    pool_pairs(*finished(j - 2))
                if now is not None and now[0] in CONV:
                    add_tap(j, 2)
                if now is not None and now[0] == 4:
                    choose(j)
                if 1 <= j + 2 < PAIRS:
                    quantise_x(2 * (j + 2))
                    quantise_x(2 * (j + 2) + 1)

                if 0 <= j + 2 < len(steps):
                    multiply(j + 2)
                if finished(j - 3) is not None:
                    turn(*finished(j - 3))
                if 1 <= j + 4 < PAIRS:
                    transpose_x(2 * (j + 4))
                    transpose_x(2 * (j + 4) + 1)

                if 0 <= j + 1 < len(steps):
                    leave_psum(j + 1)
                if 1 <= j + 3 < PAIRS:
                    regroup_x(2 * (j + 3))
                    regroup_x(2 * (j + 3) + 1)
                if 0 <= j - 1 < len(steps) and steps[j - 1][0] == 4:
                    normalise(j - 1)
                if finished(j - 4) is not None:
                    shuffle_out(*finished(j - 4))
